import numpy as np
import ml_dtypes

BF16 = ml_dtypes.bfloat16


def bf(x):
    return np.asarray(x, np.float32).astype(BF16)


def f32(x):
    return np.asarray(x, np.float32)


def f64(x):
    return np.asarray(x).astype(np.float64)


def striped(idx):
    return np.tile(idx.reshape(-1, 16).T, (8, 1))


C, K, S, N = 256, 128, 4096, 2048
THETA = 10000.0


def setup_inputs():
    inv = 1.0 / THETA ** (np.arange(K) / K)
    t0 = np.random.uniform(0.0, S)
    ang = inv[:, None] * (np.arange(S) + t0)[None, :]
    cs = bf(np.concatenate([np.cos(ang), np.sin(ang)], axis=0))
    x = bf(np.random.standard_normal((C, N)))
    idx = np.random.permutation(np.tile(np.arange(S), 2))[:N]
    return {"cs": cs, "x": x, "offs": striped(idx)}


def reference(cs, x, offs):
    idx = offs[:16].T.reshape(-1)
    t = f64(cs)[:, idx]
    co, si = t[:K], t[K:]
    xa, xb = f64(x)[:K], f64(x)[K:]
    return np.concatenate([co * xa - si * xb, si * xa + co * xb], axis=0)

@@ -1,0 +1,53 @@
+import concourse.mybir as mybir
+
+P = 128
+S = 4096
+N = 2048
+
+BF16 = mybir.dt.bfloat16
+F32 = mybir.dt.float32
+U16 = mybir.dt.uint16
+MULT = mybir.AluOpType.mult
+ADD = mybir.AluOpType.add
+SUBTRACT = mybir.AluOpType.subtract
+
+
+def tile_myrotarypositionalembedding_kernel(tc, cs, x, offs, out):
+    nc = tc.nc
+    with tc.tile_pool(name="held", bufs=1) as held:
+        offsets = held.tile([P, N // 16], U16, name="offsets")
+        nc.sync.dma_start(offsets[:], offs)
+
+        cos_bf = held.tile([P, S], BF16, name="cos_bf")
+        sin_bf = held.tile([P, S], BF16, name="sin_bf")
+        xa_bf = held.tile([P, N], BF16, name="xa_bf")
+        xb_bf = held.tile([P, N], BF16, name="xb_bf")
+        nc.sync.dma_start(cos_bf[:], cs[0:P, :])
+        nc.scalar.dma_start(xa_bf[:], x[0:P, :])
+        nc.scalar.dma_start(xb_bf[:], x[P : 2 * P, :])
+        nc.sync.dma_start(sin_bf[:], cs[P : 2 * P, :])
+
+        cos = held.tile([P, S], F32, name="cos")
+        sin = held.tile([P, S], F32, name="sin")
+        xa = held.tile([P, N], F32, name="xa")
+        xb = held.tile([P, N], F32, name="xb")
+        nc.vector.tensor_copy(cos[:], cos_bf[:])
+        nc.scalar.copy(xa[:], xa_bf[:])
+        nc.scalar.copy(xb[:], xb_bf[:])
+        nc.scalar.copy(sin[:], sin_bf[:])
+
+        cos_xa = held.tile([P, N], F32, name="cos_xa")
+        cos_xb = held.tile([P, N], F32, name="cos_xb")
+        sin_xa = held.tile([P, N], F32, name="sin_xa")
+        sin_xb = held.tile([P, N], F32, name="sin_xb")
+        first = held.tile([P, N], F32, name="first")
+        second = held.tile([P, N], F32, name="second")
+
+        nc.vector.tensor_tensor(cos_xa[:], cos[:].indirect(offsets[:]), xa[:], MULT)
+        nc.vector.tensor_tensor(cos_xb[:], cos[:].indirect(offsets[:]), xb[:], MULT)
+        nc.vector.tensor_tensor(sin_xb[:], sin[:].indirect(offsets[:]), xb[:], MULT)
+        nc.vector.tensor_tensor(first[:], cos_xa[:], sin_xb[:], SUBTRACT)
+        nc.sync.dma_start(out[0:P, :], first[:])
+        nc.vector.tensor_tensor(sin_xa[:], sin[:].indirect(offsets[:]), xa[:], MULT)
+        nc.vector.tensor_tensor(second[:], sin_xa[:], cos_xb[:], ADD)
+        nc.sync.dma_start(out[P : 2 * P, :], second[:])

@@ -3,6 +3,9 @@ import concourse.mybir as mybir
 P = 128
 S = 4096
 N = 2048
+CHUNK = 1024
+PIECE = 512
+N_PIECES = N // PIECE
 
 BF16 = mybir.dt.bfloat16
 F32 = mybir.dt.float32
@@ -10,6 +13,14 @@ U16 = mybir.dt.uint16
 MULT = mybir.AluOpType.mult
 ADD = mybir.AluOpType.add
 SUBTRACT = mybir.AluOpType.subtract
+
+
+def chunk(c):
+    return slice(c * CHUNK, (c + 1) * CHUNK)
+
+
+def piece(h):
+    return slice(h * PIECE, (h + 1) * PIECE)
 
 
 def tile_myrotarypositionalembedding_kernel(tc, cs, x, offs, out):
@@ -22,19 +33,28 @@ def tile_myrotarypositionalembedding_kernel(tc, cs, x, offs, out):
         sin_bf = held.tile([P, S], BF16, name="sin_bf")
         xa_bf = held.tile([P, N], BF16, name="xa_bf")
         xb_bf = held.tile([P, N], BF16, name="xb_bf")
-        nc.sync.dma_start(cos_bf[:], cs[0:P, :])
-        nc.scalar.dma_start(xa_bf[:], x[0:P, :])
-        nc.scalar.dma_start(xb_bf[:], x[P : 2 * P, :])
-        nc.sync.dma_start(sin_bf[:], cs[P : 2 * P, :])
+        queues = (nc.sync, nc.scalar)
+        nc.scalar.dma_start(xa_bf[:, chunk(0)], x[0:P, chunk(0)])
+        for c in range(S // CHUNK):
+            queues[c % 2].dma_start(cos_bf[:, chunk(c)], cs[0:P, chunk(c)])
+        nc.sync.dma_start(xa_bf[:, chunk(1)], x[0:P, chunk(1)])
+        for c in range(N // CHUNK):
+            queues[c % 2].dma_start(xb_bf[:, chunk(c)], x[P : 2 * P, chunk(c)])
+        for c in range(S // CHUNK):
+            queues[c % 2].dma_start(sin_bf[:, chunk(c)], cs[P : 2 * P, chunk(c)])
 
         cos = held.tile([P, S], F32, name="cos")
         sin = held.tile([P, S], F32, name="sin")
         xa = held.tile([P, N], F32, name="xa")
         xb = held.tile([P, N], F32, name="xb")
-        nc.vector.tensor_copy(cos[:], cos_bf[:])
-        nc.scalar.copy(xa[:], xa_bf[:])
-        nc.scalar.copy(xb[:], xb_bf[:])
-        nc.scalar.copy(sin[:], sin_bf[:])
+        for c in range(S // CHUNK):
+            nc.vector.tensor_copy(cos[:, chunk(c)], cos_bf[:, chunk(c)])
+        for c in range(N // CHUNK):
+            nc.scalar.copy(xa[:, chunk(c)], xa_bf[:, chunk(c)])
+        for c in range(N // CHUNK):
+            nc.scalar.copy(xb[:, chunk(c)], xb_bf[:, chunk(c)])
+        for c in range(S // CHUNK):
+            nc.scalar.copy(sin[:, chunk(c)], sin_bf[:, chunk(c)])
 
         cos_xa = held.tile([P, N], F32, name="cos_xa")
         cos_xb = held.tile([P, N], F32, name="cos_xb")
@@ -43,11 +63,17 @@ def tile_myrotarypositionalembedding_kernel(tc, cs, x, offs, out):
         first = held.tile([P, N], F32, name="first")
         second = held.tile([P, N], F32, name="second")
 
-        nc.vector.tensor_tensor(cos_xa[:], cos[:].indirect(offsets[:]), xa[:], MULT)
-        nc.vector.tensor_tensor(cos_xb[:], cos[:].indirect(offsets[:]), xb[:], MULT)
-        nc.vector.tensor_tensor(sin_xb[:], sin[:].indirect(offsets[:]), xb[:], MULT)
-        nc.vector.tensor_tensor(first[:], cos_xa[:], sin_xb[:], SUBTRACT)
-        nc.sync.dma_start(out[0:P, :], first[:])
-        nc.vector.tensor_tensor(sin_xa[:], sin[:].indirect(offsets[:]), xa[:], MULT)
-        nc.vector.tensor_tensor(second[:], sin_xa[:], cos_xb[:], ADD)
-        nc.sync.dma_start(out[P : 2 * P, :], second[:])
+        def looked_up(table, h):
+            return table[:].indirect(offsets[:, h * (PIECE // 16) : (h + 1) * (PIECE // 16)])
+
+        for h in range(N_PIECES):
+            nc.vector.tensor_tensor(cos_xa[:, piece(h)], looked_up(cos, h), xa[:, piece(h)], MULT)
+        for h in range(N_PIECES):
+            nc.vector.tensor_tensor(cos_xb[:, piece(h)], looked_up(cos, h), xb[:, piece(h)], MULT)
+        for h in range(N_PIECES):
+            nc.vector.tensor_tensor(sin_xb[:, piece(h)], looked_up(sin, h), xb[:, piece(h)], MULT)
+            nc.vector.tensor_tensor(first[:, piece(h)], cos_xa[:, piece(h)], sin_xb[:, piece(h)], SUBTRACT)
+            nc.sync.dma_start(out[0:P, piece(h)], first[:, piece(h)])
+            nc.vector.tensor_tensor(sin_xa[:, piece(h)], looked_up(sin, h), xa[:, piece(h)], MULT)
+            nc.vector.tensor_tensor(second[:, piece(h)], sin_xa[:, piece(h)], cos_xb[:, piece(h)], ADD)
+            nc.sync.dma_start(out[P : 2 * P, piece(h)], second[:, piece(h)])

@@ -1,3 +1,4 @@
+import concourse.masks as masks
 import concourse.mybir as mybir
 
 P = 128
@@ -11,8 +12,6 @@ BF16 = mybir.dt.bfloat16
 F32 = mybir.dt.float32
 U16 = mybir.dt.uint16
 MULT = mybir.AluOpType.mult
-ADD = mybir.AluOpType.add
-SUBTRACT = mybir.AluOpType.subtract
 
 
 def chunk(c):
@@ -25,7 +24,10 @@ def piece(h):
 
 def tile_myrotarypositionalembedding_kernel(tc, cs, x, offs, out):
     nc = tc.nc
-    with tc.tile_pool(name="held", bufs=1) as held:
+    with (
+        tc.tile_pool(name="held", bufs=1) as held,
+        tc.psum_pool(name="sums", bufs=1) as sums,
+    ):
         offsets = held.tile([P, N // 16], U16, name="offsets")
         nc.sync.dma_start(offsets[:], offs)
 
@@ -42,6 +44,11 @@ def tile_myrotarypositionalembedding_kernel(tc, cs, x, offs, out):
             queues[c % 2].dma_start(xb_bf[:, chunk(c)], x[P : 2 * P, chunk(c)])
         for c in range(S // CHUNK):
             queues[c % 2].dma_start(sin_bf[:, chunk(c)], cs[P : 2 * P, chunk(c)])
+
+        plus = held.tile([P, P], F32, name="plus")
+        minus = held.tile([P, P], F32, name="minus")
+        masks.make_identity(nc, plus[:])
+        nc.scalar.mul(minus[:], plus[:], -1.0)
 
         cos = held.tile([P, S], F32, name="cos")
         sin = held.tile([P, S], F32, name="sin")
@@ -62,18 +69,24 @@ def tile_myrotarypositionalembedding_kernel(tc, cs, x, offs, out):
         sin_xb = held.tile([P, N], F32, name="sin_xb")
         first = held.tile([P, N], F32, name="first")
         second = held.tile([P, N], F32, name="second")
+        first_sum = [sums.tile([P, PIECE], F32, name=f"first_sum{h}") for h in range(N_PIECES)]
+        second_sum = [sums.tile([P, PIECE], F32, name=f"second_sum{h}") for h in range(N_PIECES)]
 
         def looked_up(table, h):
             return table[:].indirect(offsets[:, h * (PIECE // 16) : (h + 1) * (PIECE // 16)])
 
         for h in range(N_PIECES):
             nc.vector.tensor_tensor(cos_xa[:, piece(h)], looked_up(cos, h), xa[:, piece(h)], MULT)
+            nc.tensor.matmul(first_sum[h][:], plus[:], cos_xa[:, piece(h)], start=True, stop=False)
         for h in range(N_PIECES):
             nc.vector.tensor_tensor(cos_xb[:, piece(h)], looked_up(cos, h), xb[:, piece(h)], MULT)
+            nc.tensor.matmul(second_sum[h][:], plus[:], cos_xb[:, piece(h)], start=True, stop=False)
         for h in range(N_PIECES):
             nc.vector.tensor_tensor(sin_xb[:, piece(h)], looked_up(sin, h), xb[:, piece(h)], MULT)
-            nc.vector.tensor_tensor(first[:, piece(h)], cos_xa[:, piece(h)], sin_xb[:, piece(h)], SUBTRACT)
+            nc.tensor.matmul(first_sum[h][:], minus[:], sin_xb[:, piece(h)], start=False, stop=True)
+            nc.scalar.copy(first[:, piece(h)], first_sum[h][:])
             nc.sync.dma_start(out[0:P, piece(h)], first[:, piece(h)])
             nc.vector.tensor_tensor(sin_xa[:, piece(h)], looked_up(sin, h), xa[:, piece(h)], MULT)
-            nc.vector.tensor_tensor(second[:, piece(h)], sin_xa[:, piece(h)], cos_xb[:, piece(h)], ADD)
+            nc.tensor.matmul(second_sum[h][:], plus[:], sin_xa[:, piece(h)], start=False, stop=True)
+            nc.scalar.copy(second[:, piece(h)], second_sum[h][:])
             nc.sync.dma_start(out[P : 2 * P, piece(h)], second[:, piece(h)])

@@ -7,11 +7,14 @@ N = 2048
 CHUNK = 1024
 PIECE = 512
 N_PIECES = N // PIECE
+LAST = N_PIECES - 1
 
 BF16 = mybir.dt.bfloat16
 F32 = mybir.dt.float32
 U16 = mybir.dt.uint16
 MULT = mybir.AluOpType.mult
+ADD = mybir.AluOpType.add
+SUBTRACT = mybir.AluOpType.subtract
 
 
 def chunk(c):
@@ -35,15 +38,15 @@ def tile_myrotarypositionalembedding_kernel(tc, cs, x, offs, out):
         sin_bf = held.tile([P, S], BF16, name="sin_bf")
         xa_bf = held.tile([P, N], BF16, name="xa_bf")
         xb_bf = held.tile([P, N], BF16, name="xb_bf")
+        nc.sync.dma_start(xa_bf[:, chunk(0)], x[0:P, chunk(0)])
         queues = (nc.sync, nc.scalar)
-        nc.scalar.dma_start(xa_bf[:, chunk(0)], x[0:P, chunk(0)])
         for c in range(S // CHUNK):
             queues[c % 2].dma_start(cos_bf[:, chunk(c)], cs[0:P, chunk(c)])
         nc.sync.dma_start(xa_bf[:, chunk(1)], x[0:P, chunk(1)])
         for c in range(N // CHUNK):
-            queues[c % 2].dma_start(xb_bf[:, chunk(c)], x[P : 2 * P, chunk(c)])
+            nc.sync.dma_start(xb_bf[:, chunk(c)], x[P : 2 * P, chunk(c)])
         for c in range(S // CHUNK):
-            queues[c % 2].dma_start(sin_bf[:, chunk(c)], cs[P : 2 * P, chunk(c)])
+            nc.sync.dma_start(sin_bf[:, chunk(c)], cs[P : 2 * P, chunk(c)])
 
         plus = held.tile([P, P], F32, name="plus")
         minus = held.tile([P, P], F32, name="minus")
@@ -54,10 +57,10 @@ def tile_myrotarypositionalembedding_kernel(tc, cs, x, offs, out):
         sin = held.tile([P, S], F32, name="sin")
         xa = held.tile([P, N], F32, name="xa")
         xb = held.tile([P, N], F32, name="xb")
+        nc.vector.tensor_copy(xa[:, chunk(0)], xa_bf[:, chunk(0)])
         for c in range(S // CHUNK):
             nc.vector.tensor_copy(cos[:, chunk(c)], cos_bf[:, chunk(c)])
-        for c in range(N // CHUNK):
-            nc.scalar.copy(xa[:, chunk(c)], xa_bf[:, chunk(c)])
+        nc.scalar.copy(xa[:, chunk(1)], xa_bf[:, chunk(1)])
         for c in range(N // CHUNK):
             nc.scalar.copy(xb[:, chunk(c)], xb_bf[:, chunk(c)])
         for c in range(S // CHUNK):
@@ -69,19 +72,21 @@ def tile_myrotarypositionalembedding_kernel(tc, cs, x, offs, out):
         sin_xb = held.tile([P, N], F32, name="sin_xb")
         first = held.tile([P, N], F32, name="first")
         second = held.tile([P, N], F32, name="second")
-        first_sum = [sums.tile([P, PIECE], F32, name=f"first_sum{h}") for h in range(N_PIECES)]
-        second_sum = [sums.tile([P, PIECE], F32, name=f"second_sum{h}") for h in range(N_PIECES)]
+        first_sum = [sums.tile([P, PIECE], F32, name=f"first_sum{h}") for h in range(LAST)]
+        second_sum = [sums.tile([P, PIECE], F32, name=f"second_sum{h}") for h in range(LAST)]
 
         def looked_up(table, h):
             return table[:].indirect(offsets[:, h * (PIECE // 16) : (h + 1) * (PIECE // 16)])
 
         for h in range(N_PIECES):
             nc.vector.tensor_tensor(cos_xa[:, piece(h)], looked_up(cos, h), xa[:, piece(h)], MULT)
-            nc.tensor.matmul(first_sum[h][:], plus[:], cos_xa[:, piece(h)], start=True, stop=False)
+            if h != LAST:
+                nc.tensor.matmul(first_sum[h][:], plus[:], cos_xa[:, piece(h)], start=True, stop=False)
         for h in range(N_PIECES):
             nc.vector.tensor_tensor(cos_xb[:, piece(h)], looked_up(cos, h), xb[:, piece(h)], MULT)
-            nc.tensor.matmul(second_sum[h][:], plus[:], cos_xb[:, piece(h)], start=True, stop=False)
-        for h in range(N_PIECES):
+            if h != LAST:
+                nc.tensor.matmul(second_sum[h][:], plus[:], cos_xb[:, piece(h)], start=True, stop=False)
+        for h in range(LAST):
             nc.vector.tensor_tensor(sin_xb[:, piece(h)], looked_up(sin, h), xb[:, piece(h)], MULT)
             nc.tensor.matmul(first_sum[h][:], minus[:], sin_xb[:, piece(h)], start=False, stop=True)
             nc.scalar.copy(first[:, piece(h)], first_sum[h][:])
@@ -90,3 +95,9 @@ def tile_myrotarypositionalembedding_kernel(tc, cs, x, offs, out):
             nc.tensor.matmul(second_sum[h][:], plus[:], sin_xa[:, piece(h)], start=False, stop=True)
             nc.scalar.copy(second[:, piece(h)], second_sum[h][:])
             nc.sync.dma_start(out[P : 2 * P, piece(h)], second[:, piece(h)])
+        nc.vector.tensor_tensor(sin_xb[:, piece(LAST)], looked_up(sin, LAST), xb[:, piece(LAST)], MULT)
+        nc.vector.tensor_tensor(first[:, piece(LAST)], cos_xa[:, piece(LAST)], sin_xb[:, piece(LAST)], SUBTRACT)
+        nc.sync.dma_start(out[0:P, piece(LAST)], first[:, piece(LAST)])
+        nc.vector.tensor_tensor(sin_xa[:, piece(LAST)], looked_up(sin, LAST), xa[:, piece(LAST)], MULT)
+        nc.vector.tensor_tensor(second[:, piece(LAST)], sin_xa[:, piece(LAST)], cos_xb[:, piece(LAST)], ADD)
+        nc.sync.dma_start(out[P : 2 * P, piece(LAST)], second[:, piece(LAST)])

@@ -39,9 +39,8 @@ def tile_myrotarypositionalembedding_kernel(tc, cs, x, offs, out):
         xa_bf = held.tile([P, N], BF16, name="xa_bf")
         xb_bf = held.tile([P, N], BF16, name="xb_bf")
         nc.sync.dma_start(xa_bf[:, chunk(0)], x[0:P, chunk(0)])
-        queues = (nc.sync, nc.scalar)
         for c in range(S // CHUNK):
-            queues[c % 2].dma_start(cos_bf[:, chunk(c)], cs[0:P, chunk(c)])
+            nc.sync.dma_start(cos_bf[:, chunk(c)], cs[0:P, chunk(c)])
         nc.sync.dma_start(xa_bf[:, chunk(1)], x[0:P, chunk(1)])
         for c in range(N // CHUNK):
             nc.sync.dma_start(xb_bf[:, chunk(c)], x[P : 2 * P, chunk(c)])

@@ -7,14 +7,11 @@ N = 2048
 CHUNK = 1024
 PIECE = 512
 N_PIECES = N // PIECE
-LAST = N_PIECES - 1
 
 BF16 = mybir.dt.bfloat16
 F32 = mybir.dt.float32
 U16 = mybir.dt.uint16
 MULT = mybir.AluOpType.mult
-ADD = mybir.AluOpType.add
-SUBTRACT = mybir.AluOpType.subtract
 
 
 def chunk(c):
@@ -71,21 +68,19 @@ def tile_myrotarypositionalembedding_kernel(tc, cs, x, offs, out):
         sin_xb = held.tile([P, N], F32, name="sin_xb")
         first = held.tile([P, N], F32, name="first")
         second = held.tile([P, N], F32, name="second")
-        first_sum = [sums.tile([P, PIECE], F32, name=f"first_sum{h}") for h in range(LAST)]
-        second_sum = [sums.tile([P, PIECE], F32, name=f"second_sum{h}") for h in range(LAST)]
+        first_sum = [sums.tile([P, PIECE], F32, name=f"first_sum{h}") for h in range(N_PIECES)]
+        second_sum = [sums.tile([P, PIECE], F32, name=f"second_sum{h}") for h in range(N_PIECES)]
 
         def looked_up(table, h):
             return table[:].indirect(offsets[:, h * (PIECE // 16) : (h + 1) * (PIECE // 16)])
 
         for h in range(N_PIECES):
             nc.vector.tensor_tensor(cos_xa[:, piece(h)], looked_up(cos, h), xa[:, piece(h)], MULT)
-            if h != LAST:
-                nc.tensor.matmul(first_sum[h][:], plus[:], cos_xa[:, piece(h)], start=True, stop=False)
+            nc.tensor.matmul(first_sum[h][:], plus[:], cos_xa[:, piece(h)], start=True, stop=False)
         for h in range(N_PIECES):
             nc.vector.tensor_tensor(cos_xb[:, piece(h)], looked_up(cos, h), xb[:, piece(h)], MULT)
-            if h != LAST:
-                nc.tensor.matmul(second_sum[h][:], plus[:], cos_xb[:, piece(h)], start=True, stop=False)
-        for h in range(LAST):
+            nc.tensor.matmul(second_sum[h][:], plus[:], cos_xb[:, piece(h)], start=True, stop=False)
+        for h in range(N_PIECES):
             nc.vector.tensor_tensor(sin_xb[:, piece(h)], looked_up(sin, h), xb[:, piece(h)], MULT)
             nc.tensor.matmul(first_sum[h][:], minus[:], sin_xb[:, piece(h)], start=False, stop=True)
             nc.scalar.copy(first[:, piece(h)], first_sum[h][:])
@@ -94,9 +89,3 @@ def tile_myrotarypositionalembedding_kernel(tc, cs, x, offs, out):
             nc.tensor.matmul(second_sum[h][:], plus[:], sin_xa[:, piece(h)], start=False, stop=True)
             nc.scalar.copy(second[:, piece(h)], second_sum[h][:])
             nc.sync.dma_start(out[P : 2 * P, piece(h)], second[:, piece(h)])
-        nc.vector.tensor_tensor(sin_xb[:, piece(LAST)], looked_up(sin, LAST), xb[:, piece(LAST)], MULT)
-        nc.vector.tensor_tensor(first[:, piece(LAST)], cos_xa[:, piece(LAST)], sin_xb[:, piece(LAST)], SUBTRACT)
-        nc.sync.dma_start(out[0:P, piece(LAST)], first[:, piece(LAST)])
-        nc.vector.tensor_tensor(sin_xa[:, piece(LAST)], looked_up(sin, LAST), xa[:, piece(LAST)], MULT)
-        nc.vector.tensor_tensor(second[:, piece(LAST)], sin_xa[:, piece(LAST)], cos_xb[:, piece(LAST)], ADD)
-        nc.sync.dma_start(out[P : 2 * P, piece(LAST)], second[:, piece(LAST)])

@@ -5,6 +5,7 @@ P = 128
 S = 4096
 N = 2048
 CHUNK = 1024
+VECTOR_SHARE = 640
 PIECE = 512
 N_PIECES = N // PIECE
 
@@ -55,7 +56,9 @@ def tile_myrotarypositionalembedding_kernel(tc, cs, x, offs, out):
         xb = held.tile([P, N], F32, name="xb")
         nc.vector.tensor_copy(xa[:, chunk(0)], xa_bf[:, chunk(0)])
         for c in range(S // CHUNK):
-            nc.vector.tensor_copy(cos[:, chunk(c)], cos_bf[:, chunk(c)])
+            split = c * CHUNK + VECTOR_SHARE
+            nc.vector.tensor_copy(cos[:, c * CHUNK : split], cos_bf[:, c * CHUNK : split])
+            nc.scalar.copy(cos[:, split : (c + 1) * CHUNK], cos_bf[:, split : (c + 1) * CHUNK])
         nc.scalar.copy(xa[:, chunk(1)], xa_bf[:, chunk(1)])
         for c in range(N // CHUNK):
             nc.scalar.copy(xb[:, chunk(c)], xb_bf[:, chunk(c)])

@@ -5,7 +5,7 @@ P = 128
 S = 4096
 N = 2048
 CHUNK = 1024
-VECTOR_SHARE = 640
+COS_LOADS = ((0, 2048), (2048, 1024), (3072, 1024))
 PIECE = 512
 N_PIECES = N // PIECE
 
@@ -30,15 +30,16 @@ def tile_myrotarypositionalembedding_kernel(tc, cs, x, offs, out):
         tc.psum_pool(name="sums", bufs=1) as sums,
     ):
         offsets = held.tile([P, N // 16], U16, name="offsets")
-        nc.sync.dma_start(offsets[:], offs)
 
         cos_bf = held.tile([P, S], BF16, name="cos_bf")
         sin_bf = held.tile([P, S], BF16, name="sin_bf")
         xa_bf = held.tile([P, N], BF16, name="xa_bf")
         xb_bf = held.tile([P, N], BF16, name="xb_bf")
-        nc.sync.dma_start(xa_bf[:, chunk(0)], x[0:P, chunk(0)])
-        for c in range(S // CHUNK):
-            nc.sync.dma_start(cos_bf[:, chunk(c)], cs[0:P, chunk(c)])
+        for start, width in COS_LOADS:
+            nc.sync.dma_start(cos_bf[:, start : start + width], cs[0:P, start : start + width])
+        nc.sync.dma_start(xa_bf[:, piece(0)], x[0:P, piece(0)])
+        nc.sync.dma_start(offsets[:], offs)
+        nc.sync.dma_start(xa_bf[:, piece(1)], x[0:P, piece(1)])
         nc.sync.dma_start(xa_bf[:, chunk(1)], x[0:P, chunk(1)])
         for c in range(N // CHUNK):
             nc.sync.dma_start(xb_bf[:, chunk(c)], x[P : 2 * P, chunk(c)])
@@ -54,11 +55,12 @@ def tile_myrotarypositionalembedding_kernel(tc, cs, x, offs, out):
         sin = held.tile([P, S], F32, name="sin")
         xa = held.tile([P, N], F32, name="xa")
         xb = held.tile([P, N], F32, name="xb")
-        nc.vector.tensor_copy(xa[:, chunk(0)], xa_bf[:, chunk(0)])
-        for c in range(S // CHUNK):
-            split = c * CHUNK + VECTOR_SHARE
-            nc.vector.tensor_copy(cos[:, c * CHUNK : split], cos_bf[:, c * CHUNK : split])
-            nc.scalar.copy(cos[:, split : (c + 1) * CHUNK], cos_bf[:, split : (c + 1) * CHUNK])
+        for start, width in COS_LOADS:
+            split = start + width * 5 // 8
+            nc.vector.tensor_copy(cos[:, start:split], cos_bf[:, start:split])
+            nc.scalar.copy(cos[:, split : start + width], cos_bf[:, split : start + width])
+        nc.vector.tensor_copy(xa[:, piece(0)], xa_bf[:, piece(0)])
+        nc.scalar.copy(xa[:, piece(1)], xa_bf[:, piece(1)])
         nc.scalar.copy(xa[:, chunk(1)], xa_bf[:, chunk(1)])
         for c in range(N // CHUNK):
             nc.scalar.copy(xb[:, chunk(c)], xb_bf[:, chunk(c)])

@@ -5,9 +5,10 @@ P = 128
 S = 4096
 N = 2048
 CHUNK = 1024
-COS_LOADS = ((0, 2048), (2048, 1024), (3072, 1024))
+COS_LOADS = ((0, 2048), (2048, 1024), (3072, 512), (3584, 512))
 PIECE = 512
 N_PIECES = N // PIECE
+LEAD = 128
 
 BF16 = mybir.dt.bfloat16
 F32 = mybir.dt.float32
@@ -21,6 +22,9 @@ def chunk(c):
 
 def piece(h):
     return slice(h * PIECE, (h + 1) * PIECE)
+
+
+LEAD_PARTS = (slice(0, LEAD), slice(LEAD, PIECE))
 
 
 def tile_myrotarypositionalembedding_kernel(tc, cs, x, offs, out):
@@ -37,8 +41,9 @@ def tile_myrotarypositionalembedding_kernel(tc, cs, x, offs, out):
         xb_bf = held.tile([P, N], BF16, name="xb_bf")
         for start, width in COS_LOADS:
             nc.sync.dma_start(cos_bf[:, start : start + width], cs[0:P, start : start + width])
-        nc.sync.dma_start(xa_bf[:, piece(0)], x[0:P, piece(0)])
+        nc.sync.dma_start(xa_bf[:, LEAD_PARTS[0]], x[0:P, LEAD_PARTS[0]])
         nc.sync.dma_start(offsets[:], offs)
+        nc.sync.dma_start(xa_bf[:, LEAD_PARTS[1]], x[0:P, LEAD_PARTS[1]])
         nc.sync.dma_start(xa_bf[:, piece(1)], x[0:P, piece(1)])
         nc.sync.dma_start(xa_bf[:, chunk(1)], x[0:P, chunk(1)])
         for c in range(N // CHUNK):
@@ -59,7 +64,8 @@ def tile_myrotarypositionalembedding_kernel(tc, cs, x, offs, out):
             split = start + width * 5 // 8
             nc.vector.tensor_copy(cos[:, start:split], cos_bf[:, start:split])
             nc.scalar.copy(cos[:, split : start + width], cos_bf[:, split : start + width])
-        nc.vector.tensor_copy(xa[:, piece(0)], xa_bf[:, piece(0)])
+        nc.vector.tensor_copy(xa[:, LEAD_PARTS[0]], xa_bf[:, LEAD_PARTS[0]])
+        nc.scalar.copy(xa[:, LEAD_PARTS[1]], xa_bf[:, LEAD_PARTS[1]])
         nc.scalar.copy(xa[:, piece(1)], xa_bf[:, piece(1)])
         nc.scalar.copy(xa[:, chunk(1)], xa_bf[:, chunk(1)])
         for c in range(N // CHUNK):
@@ -76,21 +82,24 @@ def tile_myrotarypositionalembedding_kernel(tc, cs, x, offs, out):
         first_sum = [sums.tile([P, PIECE], F32, name=f"first_sum{h}") for h in range(N_PIECES)]
         second_sum = [sums.tile([P, PIECE], F32, name=f"second_sum{h}") for h in range(N_PIECES)]
 
-        def looked_up(table, h):
-            return table[:].indirect(offsets[:, h * (PIECE // 16) : (h + 1) * (PIECE // 16)])
+        def looked_up(table, tokens):
+            return table[:].indirect(offsets[:, tokens.start // 16 : tokens.stop // 16])
 
-        for h in range(N_PIECES):
-            nc.vector.tensor_tensor(cos_xa[:, piece(h)], looked_up(cos, h), xa[:, piece(h)], MULT)
+        for part in LEAD_PARTS:
+            nc.vector.tensor_tensor(cos_xa[:, part], looked_up(cos, part), xa[:, part], MULT)
+            nc.tensor.matmul(first_sum[0][:, part], plus[:], cos_xa[:, part], start=part.start == 0, stop=False)
+        for h in range(1, N_PIECES):
+            nc.vector.tensor_tensor(cos_xa[:, piece(h)], looked_up(cos, piece(h)), xa[:, piece(h)], MULT)
             nc.tensor.matmul(first_sum[h][:], plus[:], cos_xa[:, piece(h)], start=True, stop=False)
         for h in range(N_PIECES):
-            nc.vector.tensor_tensor(cos_xb[:, piece(h)], looked_up(cos, h), xb[:, piece(h)], MULT)
+            nc.vector.tensor_tensor(cos_xb[:, piece(h)], looked_up(cos, piece(h)), xb[:, piece(h)], MULT)
             nc.tensor.matmul(second_sum[h][:], plus[:], cos_xb[:, piece(h)], start=True, stop=False)
         for h in range(N_PIECES):
-            nc.vector.tensor_tensor(sin_xb[:, piece(h)], looked_up(sin, h), xb[:, piece(h)], MULT)
+            nc.vector.tensor_tensor(sin_xb[:, piece(h)], looked_up(sin, piece(h)), xb[:, piece(h)], MULT)
             nc.tensor.matmul(first_sum[h][:], minus[:], sin_xb[:, piece(h)], start=False, stop=True)
             nc.scalar.copy(first[:, piece(h)], first_sum[h][:])
             nc.sync.dma_start(out[0:P, piece(h)], first[:, piece(h)])
-            nc.vector.tensor_tensor(sin_xa[:, piece(h)], looked_up(sin, h), xa[:, piece(h)], MULT)
+            nc.vector.tensor_tensor(sin_xa[:, piece(h)], looked_up(sin, piece(h)), xa[:, piece(h)], MULT)
             nc.tensor.matmul(second_sum[h][:], plus[:], sin_xa[:, piece(h)], start=False, stop=True)
             nc.scalar.copy(second[:, piece(h)], second_sum[h][:])
             nc.sync.dma_start(out[P : 2 * P, piece(h)], second[:, piece(h)])

@@ -8,6 +8,7 @@ CHUNK = 1024
 COS_LOADS = ((0, 2048), (2048, 1024), (3072, 512), (3584, 512))
 PIECE = 512
 N_PIECES = N // PIECE
+HALF = PIECE // 2
 LEAD = 128
 
 BF16 = mybir.dt.bfloat16
@@ -94,12 +95,19 @@ def tile_myrotarypositionalembedding_kernel(tc, cs, x, offs, out):
         for h in range(N_PIECES):
             nc.vector.tensor_tensor(cos_xb[:, piece(h)], looked_up(cos, piece(h)), xb[:, piece(h)], MULT)
             nc.tensor.matmul(second_sum[h][:], plus[:], cos_xb[:, piece(h)], start=True, stop=False)
+        def multiply_and_close(total, sign, product, other, h):
+            step = HALF if h == N_PIECES - 1 else PIECE
+            for start in range(0, PIECE, step):
+                tokens = slice(h * PIECE + start, h * PIECE + start + step)
+                nc.vector.tensor_tensor(product[:, tokens], looked_up(sin, tokens), other[:, tokens], MULT)
+                nc.tensor.matmul(
+                    total[:, start : start + step], sign[:], product[:, tokens], start=False, stop=start + step == PIECE
+                )
+
         for h in range(N_PIECES):
-            nc.vector.tensor_tensor(sin_xb[:, piece(h)], looked_up(sin, piece(h)), xb[:, piece(h)], MULT)
-            nc.tensor.matmul(first_sum[h][:], minus[:], sin_xb[:, piece(h)], start=False, stop=True)
+            multiply_and_close(first_sum[h], minus, sin_xb, xb, h)
             nc.scalar.copy(first[:, piece(h)], first_sum[h][:])
             nc.sync.dma_start(out[0:P, piece(h)], first[:, piece(h)])
-            nc.vector.tensor_tensor(sin_xa[:, piece(h)], looked_up(sin, piece(h)), xa[:, piece(h)], MULT)
-            nc.tensor.matmul(second_sum[h][:], plus[:], sin_xa[:, piece(h)], start=False, stop=True)
+            multiply_and_close(second_sum[h], plus, sin_xa, xa, h)
             nc.scalar.copy(second[:, piece(h)], second_sum[h][:])
             nc.sync.dma_start(out[P : 2 * P, piece(h)], second[:, piece(h)])

@@ -9,6 +9,7 @@ COS_LOADS = ((0, 2048), (2048, 1024), (3072, 512), (3584, 512))
 PIECE = 512
 N_PIECES = N // PIECE
 HALF = PIECE // 2
+TAIL = 128
 LEAD = 128
 
 BF16 = mybir.dt.bfloat16
@@ -26,6 +27,9 @@ def piece(h):
 
 
 LEAD_PARTS = (slice(0, LEAD), slice(LEAD, PIECE))
+
+SECOND_TOKENS = (piece(0), piece(1), piece(2), slice(N - PIECE, N - TAIL))
+TAIL_TOKENS = slice(N - TAIL, N)
 
 
 def tile_myrotarypositionalembedding_kernel(tc, cs, x, offs, out):
@@ -83,31 +87,41 @@ def tile_myrotarypositionalembedding_kernel(tc, cs, x, offs, out):
         first_sum = [sums.tile([P, PIECE], F32, name=f"first_sum{h}") for h in range(N_PIECES)]
         second_sum = [sums.tile([P, PIECE], F32, name=f"second_sum{h}") for h in range(N_PIECES)]
 
-        def looked_up(table, tokens):
-            return table[:].indirect(offsets[:, tokens.start // 16 : tokens.stop // 16])
-
-        for part in LEAD_PARTS:
-            nc.vector.tensor_tensor(cos_xa[:, part], looked_up(cos, part), xa[:, part], MULT)
-            nc.tensor.matmul(first_sum[0][:, part], plus[:], cos_xa[:, part], start=part.start == 0, stop=False)
-        for h in range(1, N_PIECES):
-            nc.vector.tensor_tensor(cos_xa[:, piece(h)], looked_up(cos, piece(h)), xa[:, piece(h)], MULT)
-            nc.tensor.matmul(first_sum[h][:], plus[:], cos_xa[:, piece(h)], start=True, stop=False)
-        for h in range(N_PIECES):
-            nc.vector.tensor_tensor(cos_xb[:, piece(h)], looked_up(cos, piece(h)), xb[:, piece(h)], MULT)
-            nc.tensor.matmul(second_sum[h][:], plus[:], cos_xb[:, piece(h)], start=True, stop=False)
-        def multiply_and_close(total, sign, product, other, h):
-            step = HALF if h == N_PIECES - 1 else PIECE
-            for start in range(0, PIECE, step):
-                tokens = slice(h * PIECE + start, h * PIECE + start + step)
-                nc.vector.tensor_tensor(product[:, tokens], looked_up(sin, tokens), other[:, tokens], MULT)
+        def multiply_and_add(table, other, product, sign, total, tokens, step, opens):
+            for a in range(tokens.start, tokens.stop, step):
+                b = min(a + step, tokens.stop)
+                columns = table[:].indirect(offsets[:, a // 16 : b // 16])
+                nc.vector.tensor_tensor(product[:, a:b], columns, other[:, a:b], MULT)
                 nc.tensor.matmul(
-                    total[:, start : start + step], sign[:], product[:, tokens], start=False, stop=start + step == PIECE
+                    total[:, a - tokens.start : b - tokens.start],
+                    sign[:],
+                    product[:, a:b],
+                    start=opens and a == tokens.start,
+                    stop=not opens and b == tokens.stop,
                 )
 
+        def store(result, total, tokens, rows):
+            nc.scalar.copy(result[:, tokens], total[:, : tokens.stop - tokens.start])
+            nc.sync.dma_start(out[rows, tokens], result[:, tokens])
+
+        for part in LEAD_PARTS:
+            nc.vector.tensor_tensor(
+                cos_xa[:, part], cos[:].indirect(offsets[:, part.start // 16 : part.stop // 16]), xa[:, part], MULT
+            )
+            nc.tensor.matmul(first_sum[0][:, part], plus[:], cos_xa[:, part], start=part.start == 0, stop=False)
+        for h in range(1, N_PIECES):
+            multiply_and_add(cos, xa, cos_xa, plus, first_sum[h], piece(h), PIECE, opens=True)
         for h in range(N_PIECES):
-            multiply_and_close(first_sum[h], minus, sin_xb, xb, h)
-            nc.scalar.copy(first[:, piece(h)], first_sum[h][:])
-            nc.sync.dma_start(out[0:P, piece(h)], first[:, piece(h)])
-            multiply_and_close(second_sum[h], plus, sin_xa, xa, h)
-            nc.scalar.copy(second[:, piece(h)], second_sum[h][:])
-            nc.sync.dma_start(out[P : 2 * P, piece(h)], second[:, piece(h)])
+            multiply_and_add(cos, xb, cos_xb, plus, second_sum[h], SECOND_TOKENS[h], PIECE, opens=True)
+        for h in range(N_PIECES):
+            step = PIECE
+            if h == N_PIECES - 1:
+                step = HALF
+                tail_sum = sums.tile([P, PIECE], F32, name="tail_sum", tag="first_sum0")
+                multiply_and_add(cos, xb, cos_xb, plus, tail_sum, TAIL_TOKENS, TAIL, opens=True)
+            multiply_and_add(sin, xb, sin_xb, minus, first_sum[h], piece(h), step, opens=False)
+            store(first, first_sum[h], piece(h), slice(0, P))
+            multiply_and_add(sin, xa, sin_xa, plus, second_sum[h], SECOND_TOKENS[h], step, opens=False)
+            store(second, second_sum[h], SECOND_TOKENS[h], slice(P, 2 * P))
+        multiply_and_add(sin, xa, sin_xa, plus, tail_sum, TAIL_TOKENS, TAIL, opens=False)
+        store(second, tail_sum, TAIL_TOKENS, slice(P, 2 * P))

@@ -9,12 +9,13 @@ COS_LOADS = ((0, 2048), (2048, 1024), (3072, 512), (3584, 512))
 PIECE = 512
 N_PIECES = N // PIECE
 HALF = PIECE // 2
-TAIL = 128
+TAIL = 256
 LEAD = 128
 
 BF16 = mybir.dt.bfloat16
 F32 = mybir.dt.float32
 U16 = mybir.dt.uint16
+ADD = mybir.AluOpType.add
 MULT = mybir.AluOpType.mult
 
 
@@ -87,11 +88,14 @@ def tile_myrotarypositionalembedding_kernel(tc, cs, x, offs, out):
         first_sum = [sums.tile([P, PIECE], F32, name=f"first_sum{h}") for h in range(N_PIECES)]
         second_sum = [sums.tile([P, PIECE], F32, name=f"second_sum{h}") for h in range(N_PIECES)]
 
+        def multiply(table, other, product, tokens):
+            columns = table[:].indirect(offsets[:, tokens.start // 16 : tokens.stop // 16])
+            nc.vector.tensor_tensor(product[:, tokens], columns, other[:, tokens], MULT)
+
         def multiply_and_add(table, other, product, sign, total, tokens, step, opens):
             for a in range(tokens.start, tokens.stop, step):
                 b = min(a + step, tokens.stop)
-                columns = table[:].indirect(offsets[:, a // 16 : b // 16])
-                nc.vector.tensor_tensor(product[:, a:b], columns, other[:, a:b], MULT)
+                multiply(table, other, product, slice(a, b))
                 nc.tensor.matmul(
                     total[:, a - tokens.start : b - tokens.start],
                     sign[:],
@@ -100,28 +104,24 @@ def tile_myrotarypositionalembedding_kernel(tc, cs, x, offs, out):
                     stop=not opens and b == tokens.stop,
                 )
 
-        def store(result, total, tokens, rows):
+        def copy_out(result, total, tokens):
             nc.scalar.copy(result[:, tokens], total[:, : tokens.stop - tokens.start])
-            nc.sync.dma_start(out[rows, tokens], result[:, tokens])
 
         for part in LEAD_PARTS:
-            nc.vector.tensor_tensor(
-                cos_xa[:, part], cos[:].indirect(offsets[:, part.start // 16 : part.stop // 16]), xa[:, part], MULT
-            )
+            multiply(cos, xa, cos_xa, part)
             nc.tensor.matmul(first_sum[0][:, part], plus[:], cos_xa[:, part], start=part.start == 0, stop=False)
         for h in range(1, N_PIECES):
             multiply_and_add(cos, xa, cos_xa, plus, first_sum[h], piece(h), PIECE, opens=True)
         for h in range(N_PIECES):
             multiply_and_add(cos, xb, cos_xb, plus, second_sum[h], SECOND_TOKENS[h], PIECE, opens=True)
+        multiply(cos, xb, cos_xb, TAIL_TOKENS)
         for h in range(N_PIECES):
-            step = PIECE
+            multiply_and_add(sin, xb, sin_xb, minus, first_sum[h], piece(h), HALF, opens=False)
+            copy_out(first, first_sum[h], piece(h))
+            nc.sync.dma_start(out[0:P, piece(h)], first[:, piece(h)])
+            multiply_and_add(sin, xa, sin_xa, plus, second_sum[h], SECOND_TOKENS[h], HALF, opens=False)
+            copy_out(second, second_sum[h], SECOND_TOKENS[h])
             if h == N_PIECES - 1:
-                step = HALF
-                tail_sum = sums.tile([P, PIECE], F32, name="tail_sum", tag="first_sum0")
-                multiply_and_add(cos, xb, cos_xb, plus, tail_sum, TAIL_TOKENS, TAIL, opens=True)
-            multiply_and_add(sin, xb, sin_xb, minus, first_sum[h], piece(h), step, opens=False)
-            store(first, first_sum[h], piece(h), slice(0, P))
-            multiply_and_add(sin, xa, sin_xa, plus, second_sum[h], SECOND_TOKENS[h], step, opens=False)
-            store(second, second_sum[h], SECOND_TOKENS[h], slice(P, 2 * P))
-        multiply_and_add(sin, xa, sin_xa, plus, tail_sum, TAIL_TOKENS, TAIL, opens=False)
-        store(second, tail_sum, TAIL_TOKENS, slice(P, 2 * P))
+                multiply(sin, xa, sin_xa, TAIL_TOKENS)
+                nc.vector.tensor_tensor(second[:, TAIL_TOKENS], cos_xb[:, TAIL_TOKENS], sin_xa[:, TAIL_TOKENS], ADD)
+            nc.sync.dma_start(out[P : 2 * P, piece(h)], second[:, piece(h)])

@@ -9,7 +9,7 @@ COS_LOADS = ((0, 2048), (2048, 1024), (3072, 512), (3584, 512))
 PIECE = 512
 N_PIECES = N // PIECE
 HALF = PIECE // 2
-TAIL = 256
+N_BANKED = N_PIECES - 1
 LEAD = 128
 
 BF16 = mybir.dt.bfloat16
@@ -17,6 +17,7 @@ F32 = mybir.dt.float32
 U16 = mybir.dt.uint16
 ADD = mybir.AluOpType.add
 MULT = mybir.AluOpType.mult
+SUBTRACT = mybir.AluOpType.subtract
 
 
 def chunk(c):
@@ -29,8 +30,8 @@ def piece(h):
 
 LEAD_PARTS = (slice(0, LEAD), slice(LEAD, PIECE))
 
-SECOND_TOKENS = (piece(0), piece(1), piece(2), slice(N - PIECE, N - TAIL))
-TAIL_TOKENS = slice(N - TAIL, N)
+LAST_HALF = slice(N - PIECE, N - HALF)
+TAIL_HALF = slice(N - HALF, N)
 
 
 def tile_myrotarypositionalembedding_kernel(tc, cs, x, offs, out):
@@ -85,43 +86,56 @@ def tile_myrotarypositionalembedding_kernel(tc, cs, x, offs, out):
         sin_xb = held.tile([P, N], F32, name="sin_xb")
         first = held.tile([P, N], F32, name="first")
         second = held.tile([P, N], F32, name="second")
-        first_sum = [sums.tile([P, PIECE], F32, name=f"first_sum{h}") for h in range(N_PIECES)]
-        second_sum = [sums.tile([P, PIECE], F32, name=f"second_sum{h}") for h in range(N_PIECES)]
+        first_sum = [sums.tile([P, PIECE], F32, name=f"first_sum{h}") for h in range(N_BANKED)]
+        second_sum = [sums.tile([P, PIECE], F32, name=f"second_sum{h}") for h in range(N_BANKED)]
+        last_sums = sums.tile([P, PIECE], F32, name="last_sums")
+        last_first = last_sums[:, :HALF]
+        last_second = last_sums[:, HALF:]
 
         def multiply(table, other, product, tokens):
             columns = table[:].indirect(offsets[:, tokens.start // 16 : tokens.stop // 16])
             nc.vector.tensor_tensor(product[:, tokens], columns, other[:, tokens], MULT)
 
-        def multiply_and_add(table, other, product, sign, total, tokens, step, opens):
-            for a in range(tokens.start, tokens.stop, step):
-                b = min(a + step, tokens.stop)
-                multiply(table, other, product, slice(a, b))
-                nc.tensor.matmul(
-                    total[:, a - tokens.start : b - tokens.start],
-                    sign[:],
-                    product[:, a:b],
-                    start=opens and a == tokens.start,
-                    stop=not opens and b == tokens.stop,
-                )
-
-        def copy_out(result, total, tokens):
-            nc.scalar.copy(result[:, tokens], total[:, : tokens.stop - tokens.start])
+        def add_up(total, sign, product, tokens, start=False, stop=False):
+            nc.tensor.matmul(total, sign[:], product[:, tokens], start=start, stop=stop)
 
         for part in LEAD_PARTS:
             multiply(cos, xa, cos_xa, part)
-            nc.tensor.matmul(first_sum[0][:, part], plus[:], cos_xa[:, part], start=part.start == 0, stop=False)
-        for h in range(1, N_PIECES):
-            multiply_and_add(cos, xa, cos_xa, plus, first_sum[h], piece(h), PIECE, opens=True)
-        for h in range(N_PIECES):
-            multiply_and_add(cos, xb, cos_xb, plus, second_sum[h], SECOND_TOKENS[h], PIECE, opens=True)
-        multiply(cos, xb, cos_xb, TAIL_TOKENS)
-        for h in range(N_PIECES):
-            multiply_and_add(sin, xb, sin_xb, minus, first_sum[h], piece(h), HALF, opens=False)
-            copy_out(first, first_sum[h], piece(h))
+            add_up(first_sum[0][:, part], plus, cos_xa, part, start=part.start == 0)
+        for h in range(1, N_BANKED):
+            multiply(cos, xa, cos_xa, piece(h))
+            add_up(first_sum[h][:], plus, cos_xa, piece(h), start=True)
+        multiply(cos, xa, cos_xa, piece(N_BANKED))
+        add_up(last_first, plus, cos_xa, LAST_HALF, start=True)
+        for h in range(N_BANKED):
+            multiply(cos, xb, cos_xb, piece(h))
+            add_up(second_sum[h][:], plus, cos_xb, piece(h), start=True)
+        multiply(cos, xb, cos_xb, piece(N_BANKED))
+        add_up(last_second, plus, cos_xb, LAST_HALF)
+
+        def close(total, sign, product, other, h):
+            for start in range(0, PIECE, HALF):
+                tokens = slice(h * PIECE + start, h * PIECE + start + HALF)
+                multiply(sin, other, product, tokens)
+                add_up(total[:, start : start + HALF], sign, product, tokens, stop=start + HALF == PIECE)
+
+        for h in range(N_BANKED):
+            close(first_sum[h], minus, sin_xb, xb, h)
+            nc.scalar.copy(first[:, piece(h)], first_sum[h][:])
             nc.sync.dma_start(out[0:P, piece(h)], first[:, piece(h)])
-            multiply_and_add(sin, xa, sin_xa, plus, second_sum[h], SECOND_TOKENS[h], HALF, opens=False)
-            copy_out(second, second_sum[h], SECOND_TOKENS[h])
-            if h == N_PIECES - 1:
-                multiply(sin, xa, sin_xa, TAIL_TOKENS)
-                nc.vector.tensor_tensor(second[:, TAIL_TOKENS], cos_xb[:, TAIL_TOKENS], sin_xa[:, TAIL_TOKENS], ADD)
+            close(second_sum[h], plus, sin_xa, xa, h)
+            nc.scalar.copy(second[:, piece(h)], second_sum[h][:])
             nc.sync.dma_start(out[P : 2 * P, piece(h)], second[:, piece(h)])
+
+        multiply(sin, xb, sin_xb, LAST_HALF)
+        add_up(last_first, minus, sin_xb, LAST_HALF)
+        multiply(sin, xa, sin_xa, LAST_HALF)
+        add_up(last_second, plus, sin_xa, LAST_HALF, stop=True)
+        nc.scalar.copy(first[:, LAST_HALF], last_first)
+        nc.scalar.copy(second[:, LAST_HALF], last_second)
+        multiply(sin, xb, sin_xb, TAIL_HALF)
+        multiply(sin, xa, sin_xa, TAIL_HALF)
+        nc.vector.tensor_tensor(first[:, TAIL_HALF], cos_xa[:, TAIL_HALF], sin_xb[:, TAIL_HALF], SUBTRACT)
+        nc.vector.tensor_tensor(second[:, TAIL_HALF], cos_xb[:, TAIL_HALF], sin_xa[:, TAIL_HALF], ADD)
+        nc.sync.dma_start(out[0:P, piece(N_BANKED)], first[:, piece(N_BANKED)])
+        nc.sync.dma_start(out[P : 2 * P, piece(N_BANKED)], second[:, piece(N_BANKED)])

@@ -5,7 +5,8 @@ P = 128
 S = 4096
 N = 2048
 CHUNK = 1024
-COS_LOADS = ((0, 2048), (2048, 1024), (3072, 512), (3584, 512))
+COS_LOADS = ((0, 2048), (2048, 1024), (3072, 768))
+LAST_COS = slice(3840, S)
 PIECE = 512
 N_PIECES = N // PIECE
 HALF = PIECE // 2
@@ -48,6 +49,7 @@ def tile_myrotarypositionalembedding_kernel(tc, cs, x, offs, out):
         xb_bf = held.tile([P, N], BF16, name="xb_bf")
         for start, width in COS_LOADS:
             nc.sync.dma_start(cos_bf[:, start : start + width], cs[0:P, start : start + width])
+        nc.sync.dma_start(cos_bf[:, LAST_COS], cs[0:P, LAST_COS])
         nc.sync.dma_start(xa_bf[:, LEAD_PARTS[0]], x[0:P, LEAD_PARTS[0]])
         nc.sync.dma_start(offsets[:], offs)
         nc.sync.dma_start(xa_bf[:, LEAD_PARTS[1]], x[0:P, LEAD_PARTS[1]])
@@ -71,6 +73,7 @@ def tile_myrotarypositionalembedding_kernel(tc, cs, x, offs, out):
             split = start + width * 5 // 8
             nc.vector.tensor_copy(cos[:, start:split], cos_bf[:, start:split])
             nc.scalar.copy(cos[:, split : start + width], cos_bf[:, split : start + width])
+        nc.vector.tensor_copy(cos[:, LAST_COS], cos_bf[:, LAST_COS])
         nc.vector.tensor_copy(xa[:, LEAD_PARTS[0]], xa_bf[:, LEAD_PARTS[0]])
         nc.scalar.copy(xa[:, LEAD_PARTS[1]], xa_bf[:, LEAD_PARTS[1]])
         nc.scalar.copy(xa[:, piece(1)], xa_bf[:, piece(1)])
@@ -114,10 +117,11 @@ def tile_myrotarypositionalembedding_kernel(tc, cs, x, offs, out):
         add_up(last_second, plus, cos_xb, LAST_HALF)
 
         def close(total, sign, product, other, h):
-            for start in range(0, PIECE, HALF):
-                tokens = slice(h * PIECE + start, h * PIECE + start + HALF)
+            step = HALF if h == N_BANKED - 1 else PIECE
+            for start in range(0, PIECE, step):
+                tokens = slice(h * PIECE + start, h * PIECE + start + step)
                 multiply(sin, other, product, tokens)
-                add_up(total[:, start : start + HALF], sign, product, tokens, stop=start + HALF == PIECE)
+                add_up(total[:, start : start + step], sign, product, tokens, stop=start + step == PIECE)
 
         for h in range(N_BANKED):
             close(first_sum[h], minus, sin_xb, xb, h)

@@ -9,7 +9,7 @@ COS_LOADS = ((0, 2048), (2048, 1024), (3072, 768))
 LAST_COS = slice(3840, S)
 PIECE = 512
 N_PIECES = N // PIECE
-HALF = PIECE // 2
+TAIL_TOKENS = 320
 N_BANKED = N_PIECES - 1
 LEAD = 128
 
@@ -31,8 +31,8 @@ def piece(h):
 
 LEAD_PARTS = (slice(0, LEAD), slice(LEAD, PIECE))
 
-LAST_HALF = slice(N - PIECE, N - HALF)
-TAIL_HALF = slice(N - HALF, N)
+LAST = slice(N - PIECE, N - TAIL_TOKENS)
+TAIL = slice(N - TAIL_TOKENS, N)
 
 
 def tile_myrotarypositionalembedding_kernel(tc, cs, x, offs, out):
@@ -92,8 +92,9 @@ def tile_myrotarypositionalembedding_kernel(tc, cs, x, offs, out):
         first_sum = [sums.tile([P, PIECE], F32, name=f"first_sum{h}") for h in range(N_BANKED)]
         second_sum = [sums.tile([P, PIECE], F32, name=f"second_sum{h}") for h in range(N_BANKED)]
         last_sums = sums.tile([P, PIECE], F32, name="last_sums")
-        last_first = last_sums[:, :HALF]
-        last_second = last_sums[:, HALF:]
+        width = PIECE - TAIL_TOKENS
+        last_first = last_sums[:, :width]
+        last_second = last_sums[:, width : 2 * width]
 
         def multiply(table, other, product, tokens):
             columns = table[:].indirect(offsets[:, tokens.start // 16 : tokens.stop // 16])
@@ -105,41 +106,38 @@ def tile_myrotarypositionalembedding_kernel(tc, cs, x, offs, out):
         for part in LEAD_PARTS:
             multiply(cos, xa, cos_xa, part)
             add_up(first_sum[0][:, part], plus, cos_xa, part, start=part.start == 0)
-        for h in range(1, N_BANKED):
-            multiply(cos, xa, cos_xa, piece(h))
-            add_up(first_sum[h][:], plus, cos_xa, piece(h), start=True)
-        multiply(cos, xa, cos_xa, piece(N_BANKED))
-        add_up(last_first, plus, cos_xa, LAST_HALF, start=True)
-        for h in range(N_BANKED):
-            multiply(cos, xb, cos_xb, piece(h))
+        multiply(cos, xa, cos_xa, piece(1))
+        add_up(first_sum[1][:], plus, cos_xa, piece(1), start=True)
+        multiply(cos, xa, cos_xa, slice(2 * PIECE, N))
+        add_up(first_sum[2][:], plus, cos_xa, piece(2), start=True)
+        add_up(last_first, plus, cos_xa, LAST, start=True)
+        multiply(cos, xb, cos_xb, slice(0, 2 * PIECE))
+        for h in range(2):
             add_up(second_sum[h][:], plus, cos_xb, piece(h), start=True)
+        multiply(cos, xb, cos_xb, piece(2))
+        add_up(second_sum[2][:], plus, cos_xb, piece(2), start=True)
         multiply(cos, xb, cos_xb, piece(N_BANKED))
-        add_up(last_second, plus, cos_xb, LAST_HALF)
-
-        def close(total, sign, product, other, h):
-            step = HALF if h == N_BANKED - 1 else PIECE
-            for start in range(0, PIECE, step):
-                tokens = slice(h * PIECE + start, h * PIECE + start + step)
-                multiply(sin, other, product, tokens)
-                add_up(total[:, start : start + step], sign, product, tokens, stop=start + step == PIECE)
+        add_up(last_second, plus, cos_xb, LAST)
 
         for h in range(N_BANKED):
-            close(first_sum[h], minus, sin_xb, xb, h)
+            multiply(sin, xb, sin_xb, piece(h))
+            add_up(first_sum[h][:], minus, sin_xb, piece(h), stop=True)
             nc.scalar.copy(first[:, piece(h)], first_sum[h][:])
             nc.sync.dma_start(out[0:P, piece(h)], first[:, piece(h)])
-            close(second_sum[h], plus, sin_xa, xa, h)
+            multiply(sin, xa, sin_xa, piece(h))
+            add_up(second_sum[h][:], plus, sin_xa, piece(h), stop=True)
             nc.scalar.copy(second[:, piece(h)], second_sum[h][:])
             nc.sync.dma_start(out[P : 2 * P, piece(h)], second[:, piece(h)])
 
-        multiply(sin, xb, sin_xb, LAST_HALF)
-        add_up(last_first, minus, sin_xb, LAST_HALF)
-        multiply(sin, xa, sin_xa, LAST_HALF)
-        add_up(last_second, plus, sin_xa, LAST_HALF, stop=True)
-        nc.scalar.copy(first[:, LAST_HALF], last_first)
-        nc.scalar.copy(second[:, LAST_HALF], last_second)
-        multiply(sin, xb, sin_xb, TAIL_HALF)
-        multiply(sin, xa, sin_xa, TAIL_HALF)
-        nc.vector.tensor_tensor(first[:, TAIL_HALF], cos_xa[:, TAIL_HALF], sin_xb[:, TAIL_HALF], SUBTRACT)
-        nc.vector.tensor_tensor(second[:, TAIL_HALF], cos_xb[:, TAIL_HALF], sin_xa[:, TAIL_HALF], ADD)
+        multiply(sin, xb, sin_xb, LAST)
+        add_up(last_first, minus, sin_xb, LAST)
+        multiply(sin, xa, sin_xa, LAST)
+        add_up(last_second, plus, sin_xa, LAST, stop=True)
+        nc.scalar.copy(first[:, LAST], last_first)
+        nc.scalar.copy(second[:, LAST], last_second)
+        multiply(sin, xb, sin_xb, TAIL)
+        multiply(sin, xa, sin_xa, TAIL)
+        nc.vector.tensor_tensor(first[:, TAIL], cos_xa[:, TAIL], sin_xb[:, TAIL], SUBTRACT)
+        nc.vector.tensor_tensor(second[:, TAIL], cos_xb[:, TAIL], sin_xa[:, TAIL], ADD)
         nc.sync.dma_start(out[0:P, piece(N_BANKED)], first[:, piece(N_BANKED)])
         nc.sync.dma_start(out[P : 2 * P, piece(N_BANKED)], second[:, piece(N_BANKED)])

@@ -114,9 +114,8 @@ def tile_myrotarypositionalembedding_kernel(tc, cs, x, offs, out):
         multiply(cos, xb, cos_xb, slice(0, 2 * PIECE))
         for h in range(2):
             add_up(second_sum[h][:], plus, cos_xb, piece(h), start=True)
-        multiply(cos, xb, cos_xb, piece(2))
+        multiply(cos, xb, cos_xb, slice(2 * PIECE, N))
         add_up(second_sum[2][:], plus, cos_xb, piece(2), start=True)
-        multiply(cos, xb, cos_xb, piece(N_BANKED))
         add_up(last_second, plus, cos_xb, LAST)
 
         for h in range(N_BANKED):

@@ -5,7 +5,7 @@ P = 128
 S = 4096
 N = 2048
 CHUNK = 1024
-COS_LOADS = ((0, 2048), (2048, 1024), (3072, 768))
+COS_LOADS = ((0, 1024), (1024, 1024), (2048, 1024), (3072, 768))
 LAST_COS = slice(3840, S)
 PIECE = 512
 N_PIECES = N // PIECE
@@ -50,9 +50,8 @@ def tile_myrotarypositionalembedding_kernel(tc, cs, x, offs, out):
         for start, width in COS_LOADS:
             nc.sync.dma_start(cos_bf[:, start : start + width], cs[0:P, start : start + width])
         nc.sync.dma_start(cos_bf[:, LAST_COS], cs[0:P, LAST_COS])
-        nc.sync.dma_start(xa_bf[:, LEAD_PARTS[0]], x[0:P, LEAD_PARTS[0]])
+        nc.sync.dma_start(xa_bf[:, piece(0)], x[0:P, piece(0)])
         nc.sync.dma_start(offsets[:], offs)
-        nc.sync.dma_start(xa_bf[:, LEAD_PARTS[1]], x[0:P, LEAD_PARTS[1]])
         nc.sync.dma_start(xa_bf[:, piece(1)], x[0:P, piece(1)])
         nc.sync.dma_start(xa_bf[:, chunk(1)], x[0:P, chunk(1)])
         for c in range(N // CHUNK):

import concourse.masks as masks
import concourse.mybir as mybir

P = 128
S = 4096
N = 2048
CHUNK = 1024
COS_LOADS = ((0, 1024), (1024, 1024), (2048, 1024), (3072, 768))
LAST_COS = slice(3840, S)
PIECE = 512
N_PIECES = N // PIECE
TAIL_TOKENS = 320
N_BANKED = N_PIECES - 1
LEAD = 128

BF16 = mybir.dt.bfloat16
F32 = mybir.dt.float32
U16 = mybir.dt.uint16
ADD = mybir.AluOpType.add
MULT = mybir.AluOpType.mult
SUBTRACT = mybir.AluOpType.subtract


def chunk(c):
    return slice(c * CHUNK, (c + 1) * CHUNK)


def piece(h):
    return slice(h * PIECE, (h + 1) * PIECE)


LEAD_PARTS = (slice(0, LEAD), slice(LEAD, PIECE))

LAST = slice(N - PIECE, N - TAIL_TOKENS)
TAIL = slice(N - TAIL_TOKENS, N)


def tile_myrotarypositionalembedding_kernel(tc, cs, x, offs, out):
    nc = tc.nc
    with (
        tc.tile_pool(name="held", bufs=1) as held,
        tc.psum_pool(name="sums", bufs=1) as sums,
    ):
        offsets = held.tile([P, N // 16], U16, name="offsets")

        cos_bf = held.tile([P, S], BF16, name="cos_bf")
        sin_bf = held.tile([P, S], BF16, name="sin_bf")
        xa_bf = held.tile([P, N], BF16, name="xa_bf")
        xb_bf = held.tile([P, N], BF16, name="xb_bf")
        for start, width in COS_LOADS:
            nc.sync.dma_start(cos_bf[:, start : start + width], cs[0:P, start : start + width])
        nc.sync.dma_start(cos_bf[:, LAST_COS], cs[0:P, LAST_COS])
        nc.sync.dma_start(xa_bf[:, piece(0)], x[0:P, piece(0)])
        nc.sync.dma_start(offsets[:], offs)
        nc.sync.dma_start(xa_bf[:, piece(1)], x[0:P, piece(1)])
        nc.sync.dma_start(xa_bf[:, chunk(1)], x[0:P, chunk(1)])
        for c in range(N // CHUNK):
            nc.sync.dma_start(xb_bf[:, chunk(c)], x[P : 2 * P, chunk(c)])
        for c in range(S // CHUNK):
            nc.sync.dma_start(sin_bf[:, chunk(c)], cs[P : 2 * P, chunk(c)])

        plus = held.tile([P, P], F32, name="plus")
        minus = held.tile([P, P], F32, name="minus")
        masks.make_identity(nc, plus[:])
        nc.scalar.mul(minus[:], plus[:], -1.0)

        cos = held.tile([P, S], F32, name="cos")
        sin = held.tile([P, S], F32, name="sin")
        xa = held.tile([P, N], F32, name="xa")
        xb = held.tile([P, N], F32, name="xb")
        for start, width in COS_LOADS:
            split = start + width * 5 // 8
            nc.vector.tensor_copy(cos[:, start:split], cos_bf[:, start:split])
            nc.scalar.copy(cos[:, split : start + width], cos_bf[:, split : start + width])
        nc.vector.tensor_copy(cos[:, LAST_COS], cos_bf[:, LAST_COS])
        nc.vector.tensor_copy(xa[:, LEAD_PARTS[0]], xa_bf[:, LEAD_PARTS[0]])
        nc.scalar.copy(xa[:, LEAD_PARTS[1]], xa_bf[:, LEAD_PARTS[1]])
        nc.scalar.copy(xa[:, piece(1)], xa_bf[:, piece(1)])
        nc.scalar.copy(xa[:, chunk(1)], xa_bf[:, chunk(1)])
        for c in range(N // CHUNK):
            nc.scalar.copy(xb[:, chunk(c)], xb_bf[:, chunk(c)])
        for c in range(S // CHUNK):
            nc.scalar.copy(sin[:, chunk(c)], sin_bf[:, chunk(c)])

        cos_xa = held.tile([P, N], F32, name="cos_xa")
        cos_xb = held.tile([P, N], F32, name="cos_xb")
        sin_xa = held.tile([P, N], F32, name="sin_xa")
        sin_xb = held.tile([P, N], F32, name="sin_xb")
        first = held.tile([P, N], F32, name="first")
        second = held.tile([P, N], F32, name="second")
        first_sum = [sums.tile([P, PIECE], F32, name=f"first_sum{h}") for h in range(N_BANKED)]
        second_sum = [sums.tile([P, PIECE], F32, name=f"second_sum{h}") for h in range(N_BANKED)]
        last_sums = sums.tile([P, PIECE], F32, name="last_sums")
        width = PIECE - TAIL_TOKENS
        last_first = last_sums[:, :width]
        last_second = last_sums[:, width : 2 * width]

        def multiply(table, other, product, tokens):
            columns = table[:].indirect(offsets[:, tokens.start // 16 : tokens.stop // 16])
            nc.vector.tensor_tensor(product[:, tokens], columns, other[:, tokens], MULT)

        def add_up(total, sign, product, tokens, start=False, stop=False):
            nc.tensor.matmul(total, sign[:], product[:, tokens], start=start, stop=stop)

        for part in LEAD_PARTS:
            multiply(cos, xa, cos_xa, part)
            add_up(first_sum[0][:, part], plus, cos_xa, part, start=part.start == 0)
        multiply(cos, xa, cos_xa, piece(1))
        add_up(first_sum[1][:], plus, cos_xa, piece(1), start=True)
        multiply(cos, xa, cos_xa, slice(2 * PIECE, N))
        add_up(first_sum[2][:], plus, cos_xa, piece(2), start=True)
        add_up(last_first, plus, cos_xa, LAST, start=True)
        multiply(cos, xb, cos_xb, slice(0, 2 * PIECE))
        for h in range(2):
            add_up(second_sum[h][:], plus, cos_xb, piece(h), start=True)
        multiply(cos, xb, cos_xb, slice(2 * PIECE, N))
        add_up(second_sum[2][:], plus, cos_xb, piece(2), start=True)
        add_up(last_second, plus, cos_xb, LAST)

        for h in range(N_BANKED):
            multiply(sin, xb, sin_xb, piece(h))
            add_up(first_sum[h][:], minus, sin_xb, piece(h), stop=True)
            nc.scalar.copy(first[:, piece(h)], first_sum[h][:])
            nc.sync.dma_start(out[0:P, piece(h)], first[:, piece(h)])
            multiply(sin, xa, sin_xa, piece(h))
            add_up(second_sum[h][:], plus, sin_xa, piece(h), stop=True)
            nc.scalar.copy(second[:, piece(h)], second_sum[h][:])
            nc.sync.dma_start(out[P : 2 * P, piece(h)], second[:, piece(h)])

        multiply(sin, xb, sin_xb, LAST)
        add_up(last_first, minus, sin_xb, LAST)
        multiply(sin, xa, sin_xa, LAST)
        add_up(last_second, plus, sin_xa, LAST, stop=True)
        nc.scalar.copy(first[:, LAST], last_first)
        nc.scalar.copy(second[:, LAST], last_second)
        multiply(sin, xb, sin_xb, TAIL)
        multiply(sin, xa, sin_xa, TAIL)
        nc.vector.tensor_tensor(first[:, TAIL], cos_xa[:, TAIL], sin_xb[:, TAIL], SUBTRACT)
        nc.vector.tensor_tensor(second[:, TAIL], cos_xb[:, TAIL], sin_xa[:, TAIL], ADD)
        nc.sync.dma_start(out[0:P, piece(N_BANKED)], first[:, piece(N_BANKED)])
        nc.sync.dma_start(out[P : 2 * P, piece(N_BANKED)], second[:, piece(N_BANKED)])
